import numpy as np
import ml_dtypes


def mxq(x, axis, fmt="e4m3"):
    dtype, down = {"e4m3": (ml_dtypes.float8_e4m3fn, 7), "e5m2": (ml_dtypes.float8_e5m2, 14)}[fmt]
    v = np.moveaxis(np.asarray(x, np.float32).astype(ml_dtypes.bfloat16).astype(np.float64), axis, -1)
    blocks = v.reshape(v.shape[:-1] + (-1, 32))
    amax = np.abs(blocks).max(-1, keepdims=True)
    byte = np.maximum(np.where(amax > 0, np.frexp(amax)[1] - 1 + 127, 0) - down, 1)
    scale = np.exp2(byte - 127.0)
    codes = (blocks / scale).astype(np.float32).astype(dtype).astype(np.float64)
    return np.moveaxis((codes * scale).reshape(v.shape), -1, axis)


WIDE = False


def mx_kscale(k):
    if not WIDE:
        return np.ones(k)
    levels = np.array([10, -10, 5, -5, 0])
    if k % 512:
        return np.exp2(np.random.permutation(np.resize(levels, k // 32))).repeat(32)
    a = np.empty((k // 512, 16))
    for p in range(k // 512):
        a[p, :8] = np.random.permutation(np.resize(levels, 8))
        for g in range(8):
            far = levels[np.abs(levels - a[p, g]) >= 10]
            a[p, g + 8] = far[np.random.randint(len(far))]
    return np.exp2(a.ravel()).repeat(32)


BF16 = ml_dtypes.bfloat16


def bf(x):
    return np.asarray(x, np.float32).astype(BF16)


def f64(x):
    return np.asarray(x).astype(np.float64)


B, F, E, H, D0, D1 = 4096, 8, 128, 128, 64, 128
FH = F * H


def setup_inputs():
    t = mx_kscale(FH)
    tf = t.reshape(F, H)
    return {"x": bf(np.random.standard_normal((B, F, E))),
            "feat_w": bf(np.random.standard_normal((F, E, H)) / np.sqrt(E) * tf[:, None, :]),
            "feat_b": bf(np.random.standard_normal((F, H)) * 0.2 * tf),
            "trans_w": bf(np.random.standard_normal((FH, FH)) / np.sqrt(FH) / t[:, None] * t[None, :]),
            "trans_b": bf(np.random.standard_normal(FH) * 0.2 * t)}


def reference(x, feat_w, feat_b, trans_w, trans_b):
    pre = (f64(x).transpose(1, 0, 2) @ f64(feat_w)).transpose(1, 0, 2) + f64(feat_b)
    h = np.maximum(pre, 0.0)
    hf = h.reshape(B, FH)
    return np.maximum((mxq(hf, 1, "e4m3") @ mxq(f64(trans_w), 0, "e4m3")) + f64(trans_b), 0.0) + hf

@@ -1,0 +1,250 @@
+from contextlib import ExitStack
+
+import concourse.mybir as mybir
+from concourse.masks import make_identity
+
+BF16 = mybir.dt.bfloat16
+F32 = mybir.dt.float32
+U32 = mybir.dt.uint32
+U8 = mybir.dt.uint8
+FP8X4 = mybir.dt.float8_e4m3fn_x4
+ACT = mybir.ActivationFunctionType
+ALU = mybir.AluOpType
+
+P = 128
+BATCH = 4096
+FEATURES = 8
+HIDDEN = FEATURES * P
+PACK = 4
+PASS_K = P * PACK
+PASSES = HIDDEN // PASS_K
+CHUNK = 512
+ROWS = CHUNK // P
+CHUNKS = BATCH // CHUNK
+TILES = BATCH // P
+BANK = 512
+
+LAG_LAYER = 1
+LAG_ROUND = 2
+LAG_TURN = 3
+LAG_QUANT = 4
+LAG_MIX = 8
+LAG_RELU = 9
+LAG_OUT = 13
+LOAD_AHEAD = 2
+
+FLOPS = 2 * BATCH * FEATURES * P * P + 2 * BATCH * HIDDEN * HIDDEN
+
+
+def tile_dsfs_pa_t_kernel(tc, x, feat_w, feat_b, trans_w, trans_b, out):
+    nc = tc.nc
+
+    x_chunks = x.rearrange("(i p r) f e -> i p r (f e)", p=P, r=ROWS)
+    out_chunks = out.rearrange("(i p r) n -> i p r n", p=P, r=ROWS)
+    w_passes = trans_w.rearrange("(g p t) n -> g p t n", t=PACK, p=P)
+
+    with ExitStack() as ctx:
+        ctx.enter_context(tc.manual_schedule())
+        const = ctx.enter_context(tc.tile_pool(name="const", bufs=1))
+        sbuf = ctx.enter_context(tc.tile_pool(name="sbuf", bufs=3))
+        psum = ctx.enter_context(tc.psum_pool(name="psum", bufs=2))
+
+        x_rows = {}
+        x_T = {}
+        z = {}
+        h16 = {}
+        grouped = {}
+        h_codes = {}
+        h_scales = {}
+        sums = {}
+        v = {}
+
+        def load_x(chunk):
+            x_rows[chunk] = sbuf.tile([P, ROWS, HIDDEN], BF16, name="x_rows", tag="x_rows")
+            if chunk == 0:
+                for r in range(ROWS):
+                    nc.sync.dma_start(out=x_rows[0][:, r, :], in_=x_chunks[0][:, r, :])
+            else:
+                nc.sync.dma_start(out=x_rows[chunk][:], in_=x_chunks[chunk])
+
+        b1_row = const.tile([P, HIDDEN], BF16)
+        nc.vector.memset(b1_row[:], 0.0)
+        b2_rows = const.tile([P, P], BF16)
+        nc.vector.memset(b2_rows[:], 0.0)
+        ones = const.tile([P, P], BF16)
+        nc.vector.memset(ones[:], 1.0)
+        x_rows[0] = sbuf.tile([P, ROWS, HIDDEN], BF16, name="x_rows", tag="x_rows")
+        nc.sync.dma_start(out=x_rows[0][:, 0, :], in_=x_chunks[0][:, 0, :])
+        nc.sync.dma_start(out=b1_row[0:1, :], in_=feat_b.rearrange("(o f) h -> o (f h)", o=1))
+        nc.sync.dma_start(out=b2_rows[0:FEATURES, :], in_=trans_b.rearrange("(f h) -> f h", f=FEATURES))
+        feat_w_sb = const.tile([P, FEATURES, P], BF16)
+        nc.sync.dma_start(out=feat_w_sb[:], in_=feat_w.rearrange("f e h -> e f h"))
+        for r in range(1, ROWS):
+            nc.sync.dma_start(out=x_rows[0][:, r, :], in_=x_chunks[0][:, r, :])
+        w_raw = const.tile([P, PASSES, PACK, HIDDEN], BF16)
+        for g in range(PASSES):
+            nc.sync.dma_start(out=w_raw[:, g, :, :], in_=w_passes[g])
+        for chunk in range(1, LOAD_AHEAD):
+            load_x(chunk)
+
+        ident_bf16 = const.tile([P, P], BF16)
+        make_identity(nc, ident_bf16[:])
+        ident_f32 = const.tile([P, P], F32)
+        make_identity(nc, ident_f32[:])
+
+        b2_ps = psum.tile([P, P], BF16, tag="turn")
+        nc.tensor.transpose(b2_ps[:], b2_rows[:], ident_bf16[:])
+        b2_col = const.tile([P, FEATURES], F32)
+        nc.vector.tensor_copy(out=b2_col[:], in_=b2_ps[:, 0:FEATURES])
+        b1_all = const.tile([P, HIDDEN], F32)
+        for g in range(PASSES):
+            b1_ps = psum.tile([P, BANK], F32, tag="pre")
+            nc.tensor.matmul(
+                b1_ps[:], lhsT=ones[:], rhs=b1_row[:, g * BANK : (g + 1) * BANK], start=True, stop=True
+            )
+            nc.vector.tensor_copy(out=b1_all[:, g * BANK : (g + 1) * BANK], in_=b1_ps[:])
+
+        w_grouped = const.tile([P, PASSES, HIDDEN, PACK], BF16, align_bytes=64)
+        w_codes = const.tile([P, PASSES, HIDDEN], U32, align_bytes=64)
+        w_scales = const.tile([P, PASSES, HIDDEN], U8, align_bytes=64)
+
+        def regroup_w(g):
+            nc.vector.tensor_copy(
+                out=w_grouped[:, g, :, :].rearrange("p (c i) t -> p c t i", i=4),
+                in_=w_raw[:, g, :, :].rearrange("p t (c i) -> p c t i", i=4),
+            )
+
+        def quantise_w(g):
+            nc.vector.quantize_mx(
+                out=w_codes[:, g, :].bitcast(FP8X4),
+                scales=w_scales[:, g, :],
+                in_=w_grouped[:, g, :, :].rearrange("p n t -> p (n t)"),
+            )
+
+        def transpose_x(i):
+            chunk, r = divmod(i, ROWS)
+            ps = psum.tile([P, FEATURES, P], BF16, name="xT_ps", tag="turn")
+            for f in range(FEATURES):
+                nc.tensor.transpose(
+                    ps[:, f, :], x_rows[chunk][:, r, f * P : (f + 1) * P], ident_bf16[:]
+                )
+            x_T[i] = sbuf.tile([P, FEATURES, P], BF16, name="x_T", tag="x_T")
+            nc.scalar.copy(out=x_T[i][:], in_=ps[:])
+
+        def layer(i):
+            z[i] = sbuf.tile([P, HIDDEN], F32, name="z", tag="z", bufs=15)
+            for g in range(PASSES):
+                ps = psum.tile([P, BANK], F32, name="pre_ps", tag="pre")
+                for q in range(PACK):
+                    f = PACK * g + q
+                    nc.tensor.matmul(
+                        ps[:, q * P : (q + 1) * P], lhsT=x_T[i][:, f, :], rhs=feat_w_sb[:, f, :],
+                        start=True, stop=True,
+                    )
+                cols = slice(g * BANK, (g + 1) * BANK)
+                nc.vector.tensor_tensor(out=z[i][:, cols], in0=ps[:], in1=b1_all[:, cols], op=ALU.add)
+
+        def round_h(i, g):
+            if g == 0:
+                h16[i] = sbuf.tile([P, PASSES, 2, 2 * P], BF16, name="h16", tag="h16")
+            dst = h16[i][:, g, :, :].rearrange("p u (q e) -> p u q e", e=2)
+            src = z[i][:, g * PASS_K : (g + 1) * PASS_K].rearrange("p (q u e) -> p u q e", u=2, e=2)
+            if g == 1:
+                nc.vector.tensor_scalar(out=dst, in0=src, scalar1=0.0, scalar2=None, op0=ALU.max)
+            else:
+                nc.scalar.activation(out=dst, in_=src, func=ACT.Relu)
+
+        def turn_h(i):
+            ps = psum.tile([P, PASSES, 2, P], F32, name="hT_ps", tag="turn")
+            for g in range(PASSES):
+                for u in range(2):
+                    nc.tensor.transpose(
+                        ps[:, g, u, :], h16[i][:, g, u, :].bitcast(F32), ident_f32[:]
+                    )
+            grouped[i] = sbuf.tile([P, PASSES, P, 2 * 2], BF16, name="grouped", tag="grouped", align_bytes=64)
+            nc.scalar.copy(
+                out=grouped[i][:].rearrange("p g r t -> p (g r t)").bitcast(F32).rearrange("p (g r u) -> p g r u", g=PASSES, u=2),
+                in_=ps[:].rearrange("p g u r -> p g r u"),
+            )
+
+        def quantise(i):
+            chunk, r = divmod(i, ROWS)
+            if r == 0:
+                h_codes[chunk] = sbuf.tile([P, PASSES, CHUNK], U32, name="h_codes", tag="h_codes", align_bytes=64)
+                h_scales[chunk] = sbuf.tile([P, PASSES, CHUNK], U8, name="h_scales", tag="h_scales", align_bytes=64)
+            cols = slice(r * P, (r + 1) * P)
+            for g in range(PASSES):
+                nc.vector.quantize_mx(
+                    out=h_codes[chunk][:, g, cols].bitcast(FP8X4),
+                    scales=h_scales[chunk][:, g, cols],
+                    in_=grouped[i][:, g, :, :].rearrange("p r t -> p (r t)"),
+                )
+
+        def mix(i):
+            chunk, part = divmod(i, ROWS)
+            for n_tile in (2 * part, 2 * part + 1):
+                n_cols = slice(n_tile * P, (n_tile + 1) * P)
+                sums[chunk, n_tile] = psum.tile([P, CHUNK], F32, name="sums", tag="sums")
+                for g in range(PASSES):
+                    nc.tensor.matmul_mx(
+                        out=sums[chunk, n_tile][:],
+                        lhsT=w_codes[:, g, n_cols].bitcast(FP8X4),
+                        lhsT_scale=w_scales[:, g, n_cols],
+                        rhs=h_codes[chunk][:, g, :].bitcast(FP8X4),
+                        rhs_scale=h_scales[chunk][:, g, :],
+                        start=(g == 0),
+                        stop=(g == PASSES - 1),
+                    )
+
+        def relu_sums(i):
+            chunk, part = divmod(i, ROWS)
+            v[i] = sbuf.tile([P, 2, CHUNK], F32, name="v", tag="v", bufs=9)
+            for j in range(2):
+                n_tile = 2 * part + j
+                nc.scalar.activation(
+                    out=v[i][:, j, :], in_=sums[chunk, n_tile][:], func=ACT.Relu,
+                    bias=b2_col[:, n_tile : n_tile + 1], scale=1.0,
+                )
+
+        def finish(i):
+            chunk, r = divmod(i, ROWS)
+            out_rows = sbuf.tile([P, HIDDEN], F32, name="out_rows", tag="out_rows", bufs=4)
+            for g in range(PASSES):
+                ps = psum.tile([P, BANK], F32, name="out_ps", tag="out")
+                for q in range(PACK):
+                    n_tile = PACK * g + q
+                    nc.tensor.transpose(
+                        ps[:, q * P : (q + 1) * P],
+                        v[ROWS * chunk + n_tile // 2][:, n_tile % 2, r * P : (r + 1) * P],
+                        ident_f32[:],
+                    )
+                cols = slice(g * BANK, (g + 1) * BANK)
+                nc.vector.scalar_tensor_tensor(
+                    out=out_rows[:, cols], in0=z[i][:, cols], scalar=0.0, in1=ps[:],
+                    op0=ALU.max, op1=ALU.add,
+                )
+            nc.sync.dma_start(out=out_chunks[chunk][:, r, :], in_=out_rows[:])
+
+        def round_both(i):
+            for g in range(PASSES):
+                round_h(i, g)
+
+        def run(stage, step, lag):
+            if 0 <= step - lag < TILES:
+                stage(step - lag)
+
+        for step in range(TILES + LAG_OUT):
+            if step % ROWS == 0 and step // ROWS + LOAD_AHEAD < CHUNKS:
+                load_x(step // ROWS + LOAD_AHEAD)
+            run(relu_sums, step, LAG_RELU)
+            run(round_both, step, LAG_ROUND)
+            run(quantise, step, LAG_QUANT)
+            run(finish, step, LAG_OUT)
+            run(transpose_x, step, 0)
+            run(turn_h, step, LAG_TURN)
+            run(layer, step, LAG_LAYER)
+            run(mix, step, LAG_MIX)
+            if step in (2, 3):
+                regroup_w(step - 2)
+            if step in (4, 5):
+                quantise_w(step - 4)

@@ -16,22 +16,15 @@ BATCH = 4096
 FEATURES = 8
 HIDDEN = FEATURES * P
 PACK = 4
-PASS_K = P * PACK
-PASSES = HIDDEN // PASS_K
-CHUNK = 512
-ROWS = CHUNK // P
-CHUNKS = BATCH // CHUNK
+PASSES = HIDDEN // (P * PACK)
+ROWS = 4
+CHUNKS = BATCH // (P * ROWS)
 TILES = BATCH // P
+PAIR = 2 * P
 BANK = 512
-
-LAG_LAYER = 1
-LAG_ROUND = 2
-LAG_TURN = 3
-LAG_QUANT = 4
-LAG_MIX = 8
-LAG_RELU = 9
-LAG_OUT = 13
+F32_MAX = 3.4028234663852886e38
 LOAD_AHEAD = 2
+LAST_LAG = 9
 
 FLOPS = 2 * BATCH * FEATURES * P * P + 2 * BATCH * HIDDEN * HIDDEN
 
@@ -50,35 +43,37 @@ def tile_dsfs_pa_t_kernel(tc, x, feat_w, feat_b, trans_w, trans_b, out):
         psum = ctx.enter_context(tc.psum_pool(name="psum", bufs=2))
 
         x_rows = {}
+        xT_ps = {}
         x_T = {}
+        pre_ps = {}
         z = {}
         h16 = {}
+        hT_ps = {}
         grouped = {}
         h_codes = {}
         h_scales = {}
         sums = {}
         v = {}
+        out_ps = {}
 
         def load_x(chunk):
             x_rows[chunk] = sbuf.tile([P, ROWS, HIDDEN], BF16, name="x_rows", tag="x_rows")
-            if chunk == 0:
-                for r in range(ROWS):
-                    nc.sync.dma_start(out=x_rows[0][:, r, :], in_=x_chunks[0][:, r, :])
-            else:
-                nc.sync.dma_start(out=x_rows[chunk][:], in_=x_chunks[chunk])
+            nc.sync.dma_start(out=x_rows[chunk][:], in_=x_chunks[chunk])
 
-        b1_row = const.tile([P, HIDDEN], BF16)
-        nc.vector.memset(b1_row[:], 0.0)
-        b2_rows = const.tile([P, P], BF16)
-        nc.vector.memset(b2_rows[:], 0.0)
         ones = const.tile([P, P], BF16)
         nc.vector.memset(ones[:], 1.0)
+        zeros = const.tile([P, BANK], BF16)
+        nc.vector.memset(zeros[:], 0.0)
+        b_rows = const.tile([P, HIDDEN], BF16)
+        nc.vector.memset(b_rows[:], 0.0)
+        b2_rows = const.tile([P, P], BF16)
+        nc.vector.memset(b2_rows[:], 0.0)
         x_rows[0] = sbuf.tile([P, ROWS, HIDDEN], BF16, name="x_rows", tag="x_rows")
         nc.sync.dma_start(out=x_rows[0][:, 0, :], in_=x_chunks[0][:, 0, :])
-        nc.sync.dma_start(out=b1_row[0:1, :], in_=feat_b.rearrange("(o f) h -> o (f h)", o=1))
-        nc.sync.dma_start(out=b2_rows[0:FEATURES, :], in_=trans_b.rearrange("(f h) -> f h", f=FEATURES))
         feat_w_sb = const.tile([P, FEATURES, P], BF16)
         nc.sync.dma_start(out=feat_w_sb[:], in_=feat_w.rearrange("f e h -> e f h"))
+        nc.sync.dma_start(out=b_rows[0:1, :], in_=feat_b.rearrange("(o f) h -> o (f h)", o=1))
+        nc.sync.dma_start(out=b2_rows[0:FEATURES, :], in_=trans_b.rearrange("(f h) -> f h", f=FEATURES))
         for r in range(1, ROWS):
             nc.sync.dma_start(out=x_rows[0][:, r, :], in_=x_chunks[0][:, r, :])
         w_raw = const.tile([P, PASSES, PACK, HIDDEN], BF16)
@@ -92,159 +87,200 @@ def tile_dsfs_pa_t_kernel(tc, x, feat_w, feat_b, trans_w, trans_b, out):
         ident_f32 = const.tile([P, P], F32)
         make_identity(nc, ident_f32[:])
 
-        b2_ps = psum.tile([P, P], BF16, tag="turn")
-        nc.tensor.transpose(b2_ps[:], b2_rows[:], ident_bf16[:])
-        b2_col = const.tile([P, FEATURES], F32)
-        nc.vector.tensor_copy(out=b2_col[:], in_=b2_ps[:, 0:FEATURES])
         b1_all = const.tile([P, HIDDEN], F32)
-        for g in range(PASSES):
-            b1_ps = psum.tile([P, BANK], F32, tag="pre")
-            nc.tensor.matmul(
-                b1_ps[:], lhsT=ones[:], rhs=b1_row[:, g * BANK : (g + 1) * BANK], start=True, stop=True
-            )
-            nc.vector.tensor_copy(out=b1_all[:, g * BANK : (g + 1) * BANK], in_=b1_ps[:])
+        b2_col = const.tile([P, FEATURES], F32)
+
+        def spread_feat_b():
+            for g in range(PASSES):
+                cols = slice(g * BANK, (g + 1) * BANK)
+                ps = psum.tile([P, BANK], F32, name="b1_ps", tag="pre", bufs=2)
+                nc.tensor.matmul(ps[:], lhsT=ones[:], rhs=b_rows[:, cols], start=True, stop=True)
+                nc.vector.tensor_copy(out=b1_all[:, cols], in_=ps[:])
+
+        def turn_trans_b():
+            ps = psum.tile([P, P], BF16, name="b2_ps", tag="turn", bufs=2)
+            nc.tensor.transpose(ps[:], b2_rows[:], ident_bf16[:])
+            nc.vector.tensor_copy(out=b2_col[:], in_=ps[:, 0:FEATURES])
 
         w_grouped = const.tile([P, PASSES, HIDDEN, PACK], BF16, align_bytes=64)
         w_codes = const.tile([P, PASSES, HIDDEN], U32, align_bytes=64)
         w_scales = const.tile([P, PASSES, HIDDEN], U8, align_bytes=64)
 
-        def regroup_w(g):
-            nc.vector.tensor_copy(
-                out=w_grouped[:, g, :, :].rearrange("p (c i) t -> p c t i", i=4),
-                in_=w_raw[:, g, :, :].rearrange("p t (c i) -> p c t i", i=4),
-            )
+        def regroup_w(g, half, engine):
+            cols = slice(half * BANK, (half + 1) * BANK)
+            dst = w_grouped[:, g, cols, :].rearrange("p (c i) t -> p c t i", i=4)
+            src = w_raw[:, g, :, cols].rearrange("p t (c i) -> p c t i", i=4)
+            if engine == "S":
+                nc.scalar.copy(out=dst, in_=src)
+            elif engine == "G":
+                nc.gpsimd.tensor_scalar(out=dst, in0=src, scalar1=1.0, scalar2=0.0, op0=ALU.mult, op1=ALU.add)
+            else:
+                nc.vector.tensor_copy(out=dst, in_=src)
 
-        def quantise_w(g):
+        def quantise_w(g, half):
+            cols = slice(half * BANK, (half + 1) * BANK)
             nc.vector.quantize_mx(
-                out=w_codes[:, g, :].bitcast(FP8X4),
-                scales=w_scales[:, g, :],
-                in_=w_grouped[:, g, :, :].rearrange("p n t -> p (n t)"),
+                out=w_codes[:, g, cols].bitcast(FP8X4),
+                scales=w_scales[:, g, cols],
+                in_=w_grouped[:, g, cols, :].rearrange("p n t -> p (n t)"),
             )
 
-        def transpose_x(i):
+        def pe_x(i):
             chunk, r = divmod(i, ROWS)
-            ps = psum.tile([P, FEATURES, P], BF16, name="xT_ps", tag="turn")
+            xT_ps[i] = psum.tile([P, FEATURES, P], BF16, name="xT_ps", tag="turn", bufs=2)
             for f in range(FEATURES):
                 nc.tensor.transpose(
-                    ps[:, f, :], x_rows[chunk][:, r, f * P : (f + 1) * P], ident_bf16[:]
+                    xT_ps[i][:, f, :], x_rows[chunk][:, r, f * P : (f + 1) * P], ident_bf16[:]
                 )
-            x_T[i] = sbuf.tile([P, FEATURES, P], BF16, name="x_T", tag="x_T")
-            nc.scalar.copy(out=x_T[i][:], in_=ps[:])
 
-        def layer(i):
-            z[i] = sbuf.tile([P, HIDDEN], F32, name="z", tag="z", bufs=15)
+        def copy_x(i):
+            x_T[i] = sbuf.tile([P, FEATURES, P], BF16, name="x_T", tag="x_T")
+            nc.scalar.copy(out=x_T[i][:], in_=xT_ps[i][:])
+
+        def pe_layer(i):
             for g in range(PASSES):
-                ps = psum.tile([P, BANK], F32, name="pre_ps", tag="pre")
+                pre_ps[i, g] = psum.tile([P, PACK, P], F32, name="pre_ps", tag="pre", bufs=2)
                 for q in range(PACK):
                     f = PACK * g + q
                     nc.tensor.matmul(
-                        ps[:, q * P : (q + 1) * P], lhsT=x_T[i][:, f, :], rhs=feat_w_sb[:, f, :],
+                        pre_ps[i, g][:, q, :], lhsT=x_T[i][:, f, :], rhs=feat_w_sb[:, f, :],
                         start=True, stop=True,
                     )
+
+        def add_bias(i):
+            z[i] = sbuf.tile([P, HIDDEN], F32, name="z", tag="z", bufs=11)
+            for g in range(PASSES):
                 cols = slice(g * BANK, (g + 1) * BANK)
-                nc.vector.tensor_tensor(out=z[i][:, cols], in0=ps[:], in1=b1_all[:, cols], op=ALU.add)
+                nc.vector.tensor_tensor(
+                    out=z[i][:, cols], in0=pre_ps[i, g][:].rearrange("p q c -> p (q c)"), in1=b1_all[:, cols], op=ALU.add
+                )
 
-        def round_h(i, g):
-            if g == 0:
-                h16[i] = sbuf.tile([P, PASSES, 2, 2 * P], BF16, name="h16", tag="h16")
-            dst = h16[i][:, g, :, :].rearrange("p u (q e) -> p u q e", e=2)
-            src = z[i][:, g * PASS_K : (g + 1) * PASS_K].rearrange("p (q u e) -> p u q e", u=2, e=2)
-            if g == 1:
-                nc.vector.tensor_scalar(out=dst, in0=src, scalar1=0.0, scalar2=None, op0=ALU.max)
-            else:
-                nc.scalar.activation(out=dst, in_=src, func=ACT.Relu)
+        def round_h(i):
+            h16[i] = sbuf.tile([P, HIDDEN], BF16, name="h16", tag="h16")
+            for g in range(PASSES):
+                dst = h16[i][:, g * BANK : (g + 1) * BANK].rearrange("p (u q e) -> p u q e", u=2, e=2)
+                src = z[i][:, g * BANK : (g + 1) * BANK].rearrange("p (q u e) -> p u q e", u=2, e=2)
+                if g == 0:
+                    nc.scalar.activation(out=dst, in_=src, func=ACT.Relu)
+                else:
+                    nc.vector.tensor_scalar(out=dst, in0=src, scalar1=0.0, scalar2=None, op0=ALU.max)
 
-        def turn_h(i):
-            ps = psum.tile([P, PASSES, 2, P], F32, name="hT_ps", tag="turn")
+        def pe_turn(i):
+            hT_ps[i] = psum.tile([P, PASSES, 2, P], F32, name="hT_ps", tag="turn", bufs=2)
             for g in range(PASSES):
                 for u in range(2):
+                    a = (2 * g + u) * PAIR
                     nc.tensor.transpose(
-                        ps[:, g, u, :], h16[i][:, g, u, :].bitcast(F32), ident_f32[:]
+                        hT_ps[i][:, g, u, :], h16[i][:, a : a + PAIR].bitcast(F32), ident_f32[:]
                     )
-            grouped[i] = sbuf.tile([P, PASSES, P, 2 * 2], BF16, name="grouped", tag="grouped", align_bytes=64)
+
+        def copy_h(i):
+            pair, r = divmod(i, 2)
+            if r == 0:
+                grouped[pair] = sbuf.tile([P, PASSES, PAIR, PACK], BF16, name="grouped", tag="grouped", align_bytes=64)
             nc.scalar.copy(
-                out=grouped[i][:].rearrange("p g r t -> p (g r t)").bitcast(F32).rearrange("p (g r u) -> p g r u", g=PASSES, u=2),
-                in_=ps[:].rearrange("p g u r -> p g r u"),
+                out=grouped[pair][:].rearrange("p g r t -> p (g r t)").bitcast(F32).rearrange("p (g r u) -> p g r u", g=PASSES, u=2)[:, :, r * P : (r + 1) * P, :],
+                in_=hT_ps[i][:].rearrange("p g u r -> p g r u"),
             )
 
         def quantise(i):
-            chunk, r = divmod(i, ROWS)
-            if r == 0:
-                h_codes[chunk] = sbuf.tile([P, PASSES, CHUNK], U32, name="h_codes", tag="h_codes", align_bytes=64)
-                h_scales[chunk] = sbuf.tile([P, PASSES, CHUNK], U8, name="h_scales", tag="h_scales", align_bytes=64)
-            cols = slice(r * P, (r + 1) * P)
-            for g in range(PASSES):
-                nc.vector.quantize_mx(
-                    out=h_codes[chunk][:, g, cols].bitcast(FP8X4),
-                    scales=h_scales[chunk][:, g, cols],
-                    in_=grouped[i][:, g, :, :].rearrange("p r t -> p (r t)"),
-                )
+            pair, g = divmod(i, 2)
+            if g == 0:
+                h_codes[pair] = sbuf.tile([P, PASSES, PAIR], U32, name="h_codes", tag="h_codes", align_bytes=64)
+                h_scales[pair] = sbuf.tile([P, PASSES, PAIR], U8, name="h_scales", tag="h_scales", align_bytes=64)
+            nc.vector.quantize_mx(
+                out=h_codes[pair][:, g, :].bitcast(FP8X4),
+                scales=h_scales[pair][:, g, :],
+                in_=grouped[pair][:, g, :, :].rearrange("p r t -> p (r t)"),
+            )
 
-        def mix(i):
-            chunk, part = divmod(i, ROWS)
-            for n_tile in (2 * part, 2 * part + 1):
-                n_cols = slice(n_tile * P, (n_tile + 1) * P)
-                sums[chunk, n_tile] = psum.tile([P, CHUNK], F32, name="sums", tag="sums")
-                for g in range(PASSES):
-                    nc.tensor.matmul_mx(
-                        out=sums[chunk, n_tile][:],
-                        lhsT=w_codes[:, g, n_cols].bitcast(FP8X4),
-                        lhsT_scale=w_scales[:, g, n_cols],
-                        rhs=h_codes[chunk][:, g, :].bitcast(FP8X4),
-                        rhs_scale=h_scales[chunk][:, g, :],
-                        start=(g == 0),
-                        stop=(g == PASSES - 1),
-                    )
+        def pe_mix(i):
+            pair, part = divmod(i, 2)
+            for b in range(2):
+                sums[i, b] = psum.tile([P, 2, PAIR], F32, name="sums", tag="sums", bufs=2)
+                for c in range(2):
+                    n_tile = 4 * part + 2 * b + c
+                    n_cols = slice(n_tile * P, (n_tile + 1) * P)
+                    for g in range(PASSES):
+                        nc.tensor.matmul_mx(
+                            out=sums[i, b][:, c, :],
+                            lhsT=w_codes[:, g, n_cols].bitcast(FP8X4),
+                            lhsT_scale=w_scales[:, g, n_cols],
+                            rhs=h_codes[pair][:, g, :].bitcast(FP8X4),
+                            rhs_scale=h_scales[pair][:, g, :],
+                            start=(g == 0),
+                            stop=(g == PASSES - 1),
+                        )
 
         def relu_sums(i):
-            chunk, part = divmod(i, ROWS)
-            v[i] = sbuf.tile([P, 2, CHUNK], F32, name="v", tag="v", bufs=9)
-            for j in range(2):
-                n_tile = 2 * part + j
+            part = i % 2
+            v[i] = sbuf.tile([P, PACK, PAIR], F32, name="v", tag="v", bufs=4)
+            for c in range(PACK):
+                n_tile = PACK * part + c
                 nc.scalar.activation(
-                    out=v[i][:, j, :], in_=sums[chunk, n_tile][:], func=ACT.Relu,
+                    out=v[i][:, c, :], in_=sums[i, c // 2][:, c % 2, :], func=ACT.Relu,
                     bias=b2_col[:, n_tile : n_tile + 1], scale=1.0,
                 )
 
+        def pe_out(i):
+            pair, r = divmod(i, 2)
+            for g in range(PASSES):
+                out_ps[i, g] = psum.tile([P, BANK], F32, name="out_ps", tag="out", bufs=2)
+                for c in range(PACK):
+                    nc.tensor.transpose(
+                        out_ps[i, g][:, c * P : (c + 1) * P], v[2 * pair + g][:, c, r * P : (r + 1) * P], ident_f32[:]
+                    )
+
         def finish(i):
             chunk, r = divmod(i, ROWS)
-            out_rows = sbuf.tile([P, HIDDEN], F32, name="out_rows", tag="out_rows", bufs=4)
+            out_rows = sbuf.tile([P, HIDDEN], F32, name="out_rows", tag="out_rows", bufs=6)
             for g in range(PASSES):
-                ps = psum.tile([P, BANK], F32, name="out_ps", tag="out")
-                for q in range(PACK):
-                    n_tile = PACK * g + q
-                    nc.tensor.transpose(
-                        ps[:, q * P : (q + 1) * P],
-                        v[ROWS * chunk + n_tile // 2][:, n_tile % 2, r * P : (r + 1) * P],
-                        ident_f32[:],
-                    )
                 cols = slice(g * BANK, (g + 1) * BANK)
                 nc.vector.scalar_tensor_tensor(
-                    out=out_rows[:, cols], in0=z[i][:, cols], scalar=0.0, in1=ps[:],
+                    out=out_rows[:, cols], in0=z[i][:, cols], scalar=0.0, in1=out_ps[i, g][:],
                     op0=ALU.max, op1=ALU.add,
                 )
             nc.sync.dma_start(out=out_chunks[chunk][:, r, :], in_=out_rows[:])
-
-        def round_both(i):
-            for g in range(PASSES):
-                round_h(i, g)
 
         def run(stage, step, lag):
             if 0 <= step - lag < TILES:
                 stage(step - lag)
 
-        for step in range(TILES + LAG_OUT):
+        def warm(count):
+            for d in range(count):
+                ps = psum.tile([P, BANK], F32, name="warm_ps", tag="out", bufs=2)
+                nc.tensor.matmul(ps[:], lhsT=ones[:], rhs=zeros[:], start=True, stop=True)
+
+        warm(4)
+        for step in range(TILES + LAST_LAG):
             if step % ROWS == 0 and step // ROWS + LOAD_AHEAD < CHUNKS:
                 load_x(step // ROWS + LOAD_AHEAD)
-            run(relu_sums, step, LAG_RELU)
-            run(round_both, step, LAG_ROUND)
-            run(quantise, step, LAG_QUANT)
-            run(finish, step, LAG_OUT)
-            run(transpose_x, step, 0)
-            run(turn_h, step, LAG_TURN)
-            run(layer, step, LAG_LAYER)
-            run(mix, step, LAG_MIX)
-            if step in (2, 3):
-                regroup_w(step - 2)
-            if step in (4, 5):
-                quantise_w(step - 4)
+            if step < 4:
+                warm(2)
+            if step == 1:
+                spread_feat_b()
+                turn_trans_b()
+            run(round_h, step, 2)
+            run(pe_mix, step, 6)
+            run(relu_sums, step, 6)
+            run(quantise, step, 4)
+            run(pe_out, step, 9)
+            run(finish, step, 9)
+            run(pe_layer, step, 1)
+            run(add_bias, step, 1)
+            run(pe_x, step, 0)
+            run(copy_x, step, 0)
+            run(pe_turn, step, 2)
+            run(copy_h, step, 2)
+            if step == 1:
+                regroup_w(0, 0, "S")
+                regroup_w(0, 1, "V")
+            if step == 2:
+                regroup_w(1, 0, "S")
+                regroup_w(1, 1, "V")
+            if step == 3:
+                quantise_w(0, 0)
+                quantise_w(0, 1)
+            if step == 4:
+                quantise_w(1, 0)
+                quantise_w(1, 1)

@@ -24,7 +24,7 @@ PAIR = 2 * P
 BANK = 512
 F32_MAX = 3.4028234663852886e38
 LOAD_AHEAD = 2
-LAST_LAG = 9
+LAST_LAG = 8
 
 FLOPS = 2 * BATCH * FEATURES * P * P + 2 * BATCH * HIDDEN * HIDDEN
 
@@ -264,8 +264,8 @@ def tile_dsfs_pa_t_kernel(tc, x, feat_w, feat_b, trans_w, trans_b, out):
             run(pe_mix, step, 6)
             run(relu_sums, step, 6)
             run(quantise, step, 4)
-            run(pe_out, step, 9)
-            run(finish, step, 9)
+            run(pe_out, step, 8)
+            run(finish, step, 8)
             run(pe_layer, step, 1)
             run(add_bias, step, 1)
             run(pe_x, step, 0)

from contextlib import ExitStack

import concourse.mybir as mybir
from concourse.masks import make_identity

BF16 = mybir.dt.bfloat16
F32 = mybir.dt.float32
U32 = mybir.dt.uint32
U8 = mybir.dt.uint8
FP8X4 = mybir.dt.float8_e4m3fn_x4
ACT = mybir.ActivationFunctionType
ALU = mybir.AluOpType

P = 128
BATCH = 4096
FEATURES = 8
HIDDEN = FEATURES * P
PACK = 4
PASSES = HIDDEN // (P * PACK)
ROWS = 4
CHUNKS = BATCH // (P * ROWS)
TILES = BATCH // P
PAIR = 2 * P
BANK = 512
F32_MAX = 3.4028234663852886e38
LOAD_AHEAD = 2
LAST_LAG = 8

FLOPS = 2 * BATCH * FEATURES * P * P + 2 * BATCH * HIDDEN * HIDDEN


def tile_dsfs_pa_t_kernel(tc, x, feat_w, feat_b, trans_w, trans_b, out):
    nc = tc.nc

    x_chunks = x.rearrange("(i p r) f e -> i p r (f e)", p=P, r=ROWS)
    out_chunks = out.rearrange("(i p r) n -> i p r n", p=P, r=ROWS)
    w_passes = trans_w.rearrange("(g p t) n -> g p t n", t=PACK, p=P)

    with ExitStack() as ctx:
        ctx.enter_context(tc.manual_schedule())
        const = ctx.enter_context(tc.tile_pool(name="const", bufs=1))
        sbuf = ctx.enter_context(tc.tile_pool(name="sbuf", bufs=3))
        psum = ctx.enter_context(tc.psum_pool(name="psum", bufs=2))

        x_rows = {}
        xT_ps = {}
        x_T = {}
        pre_ps = {}
        z = {}
        h16 = {}
        hT_ps = {}
        grouped = {}
        h_codes = {}
        h_scales = {}
        sums = {}
        v = {}
        out_ps = {}

        def load_x(chunk):
            x_rows[chunk] = sbuf.tile([P, ROWS, HIDDEN], BF16, name="x_rows", tag="x_rows")
            nc.sync.dma_start(out=x_rows[chunk][:], in_=x_chunks[chunk])

        ones = const.tile([P, P], BF16)
        nc.vector.memset(ones[:], 1.0)
        zeros = const.tile([P, BANK], BF16)
        nc.vector.memset(zeros[:], 0.0)
        b_rows = const.tile([P, HIDDEN], BF16)
        nc.vector.memset(b_rows[:], 0.0)
        b2_rows = const.tile([P, P], BF16)
        nc.vector.memset(b2_rows[:], 0.0)
        x_rows[0] = sbuf.tile([P, ROWS, HIDDEN], BF16, name="x_rows", tag="x_rows")
        nc.sync.dma_start(out=x_rows[0][:, 0, :], in_=x_chunks[0][:, 0, :])
        feat_w_sb = const.tile([P, FEATURES, P], BF16)
        nc.sync.dma_start(out=feat_w_sb[:], in_=feat_w.rearrange("f e h -> e f h"))
        nc.sync.dma_start(out=b_rows[0:1, :], in_=feat_b.rearrange("(o f) h -> o (f h)", o=1))
        nc.sync.dma_start(out=b2_rows[0:FEATURES, :], in_=trans_b.rearrange("(f h) -> f h", f=FEATURES))
        for r in range(1, ROWS):
            nc.sync.dma_start(out=x_rows[0][:, r, :], in_=x_chunks[0][:, r, :])
        w_raw = const.tile([P, PASSES, PACK, HIDDEN], BF16)
        for g in range(PASSES):
            nc.sync.dma_start(out=w_raw[:, g, :, :], in_=w_passes[g])
        for chunk in range(1, LOAD_AHEAD):
            load_x(chunk)

        ident_bf16 = const.tile([P, P], BF16)
        make_identity(nc, ident_bf16[:])
        ident_f32 = const.tile([P, P], F32)
        make_identity(nc, ident_f32[:])

        b1_all = const.tile([P, HIDDEN], F32)
        b2_col = const.tile([P, FEATURES], F32)

        def spread_feat_b():
            for g in range(PASSES):
                cols = slice(g * BANK, (g + 1) * BANK)
                ps = psum.tile([P, BANK], F32, name="b1_ps", tag="pre", bufs=2)
                nc.tensor.matmul(ps[:], lhsT=ones[:], rhs=b_rows[:, cols], start=True, stop=True)
                nc.vector.tensor_copy(out=b1_all[:, cols], in_=ps[:])

        def turn_trans_b():
            ps = psum.tile([P, P], BF16, name="b2_ps", tag="turn", bufs=2)
            nc.tensor.transpose(ps[:], b2_rows[:], ident_bf16[:])
            nc.vector.tensor_copy(out=b2_col[:], in_=ps[:, 0:FEATURES])

        w_grouped = const.tile([P, PASSES, HIDDEN, PACK], BF16, align_bytes=64)
        w_codes = const.tile([P, PASSES, HIDDEN], U32, align_bytes=64)
        w_scales = const.tile([P, PASSES, HIDDEN], U8, align_bytes=64)

        def regroup_w(g, half, engine):
            cols = slice(half * BANK, (half + 1) * BANK)
            dst = w_grouped[:, g, cols, :].rearrange("p (c i) t -> p c t i", i=4)
            src = w_raw[:, g, :, cols].rearrange("p t (c i) -> p c t i", i=4)
            if engine == "S":
                nc.scalar.copy(out=dst, in_=src)
            elif engine == "G":
                nc.gpsimd.tensor_scalar(out=dst, in0=src, scalar1=1.0, scalar2=0.0, op0=ALU.mult, op1=ALU.add)
            else:
                nc.vector.tensor_copy(out=dst, in_=src)

        def quantise_w(g, half):
            cols = slice(half * BANK, (half + 1) * BANK)
            nc.vector.quantize_mx(
                out=w_codes[:, g, cols].bitcast(FP8X4),
                scales=w_scales[:, g, cols],
                in_=w_grouped[:, g, cols, :].rearrange("p n t -> p (n t)"),
            )

        def pe_x(i):
            chunk, r = divmod(i, ROWS)
            xT_ps[i] = psum.tile([P, FEATURES, P], BF16, name="xT_ps", tag="turn", bufs=2)
            for f in range(FEATURES):
                nc.tensor.transpose(
                    xT_ps[i][:, f, :], x_rows[chunk][:, r, f * P : (f + 1) * P], ident_bf16[:]
                )

        def copy_x(i):
            x_T[i] = sbuf.tile([P, FEATURES, P], BF16, name="x_T", tag="x_T")
            nc.scalar.copy(out=x_T[i][:], in_=xT_ps[i][:])

        def pe_layer(i):
            for g in range(PASSES):
                pre_ps[i, g] = psum.tile([P, PACK, P], F32, name="pre_ps", tag="pre", bufs=2)
                for q in range(PACK):
                    f = PACK * g + q
                    nc.tensor.matmul(
                        pre_ps[i, g][:, q, :], lhsT=x_T[i][:, f, :], rhs=feat_w_sb[:, f, :],
                        start=True, stop=True,
                    )

        def add_bias(i):
            z[i] = sbuf.tile([P, HIDDEN], F32, name="z", tag="z", bufs=11)
            for g in range(PASSES):
                cols = slice(g * BANK, (g + 1) * BANK)
                nc.vector.tensor_tensor(
                    out=z[i][:, cols], in0=pre_ps[i, g][:].rearrange("p q c -> p (q c)"), in1=b1_all[:, cols], op=ALU.add
                )

        def round_h(i):
            h16[i] = sbuf.tile([P, HIDDEN], BF16, name="h16", tag="h16")
            for g in range(PASSES):
                dst = h16[i][:, g * BANK : (g + 1) * BANK].rearrange("p (u q e) -> p u q e", u=2, e=2)
                src = z[i][:, g * BANK : (g + 1) * BANK].rearrange("p (q u e) -> p u q e", u=2, e=2)
                if g == 0:
                    nc.scalar.activation(out=dst, in_=src, func=ACT.Relu)
                else:
                    nc.vector.tensor_scalar(out=dst, in0=src, scalar1=0.0, scalar2=None, op0=ALU.max)

        def pe_turn(i):
            hT_ps[i] = psum.tile([P, PASSES, 2, P], F32, name="hT_ps", tag="turn", bufs=2)
            for g in range(PASSES):
                for u in range(2):
                    a = (2 * g + u) * PAIR
                    nc.tensor.transpose(
                        hT_ps[i][:, g, u, :], h16[i][:, a : a + PAIR].bitcast(F32), ident_f32[:]
                    )

        def copy_h(i):
            pair, r = divmod(i, 2)
            if r == 0:
                grouped[pair] = sbuf.tile([P, PASSES, PAIR, PACK], BF16, name="grouped", tag="grouped", align_bytes=64)
            nc.scalar.copy(
                out=grouped[pair][:].rearrange("p g r t -> p (g r t)").bitcast(F32).rearrange("p (g r u) -> p g r u", g=PASSES, u=2)[:, :, r * P : (r + 1) * P, :],
                in_=hT_ps[i][:].rearrange("p g u r -> p g r u"),
            )

        def quantise(i):
            pair, g = divmod(i, 2)
            if g == 0:
                h_codes[pair] = sbuf.tile([P, PASSES, PAIR], U32, name="h_codes", tag="h_codes", align_bytes=64)
                h_scales[pair] = sbuf.tile([P, PASSES, PAIR], U8, name="h_scales", tag="h_scales", align_bytes=64)
            nc.vector.quantize_mx(
                out=h_codes[pair][:, g, :].bitcast(FP8X4),
                scales=h_scales[pair][:, g, :],
                in_=grouped[pair][:, g, :, :].rearrange("p r t -> p (r t)"),
            )

        def pe_mix(i):
            pair, part = divmod(i, 2)
            for b in range(2):
                sums[i, b] = psum.tile([P, 2, PAIR], F32, name="sums", tag="sums", bufs=2)
                for c in range(2):
                    n_tile = 4 * part + 2 * b + c
                    n_cols = slice(n_tile * P, (n_tile + 1) * P)
                    for g in range(PASSES):
                        nc.tensor.matmul_mx(
                            out=sums[i, b][:, c, :],
                            lhsT=w_codes[:, g, n_cols].bitcast(FP8X4),
                            lhsT_scale=w_scales[:, g, n_cols],
                            rhs=h_codes[pair][:, g, :].bitcast(FP8X4),
                            rhs_scale=h_scales[pair][:, g, :],
                            start=(g == 0),
                            stop=(g == PASSES - 1),
                        )

        def relu_sums(i):
            part = i % 2
            v[i] = sbuf.tile([P, PACK, PAIR], F32, name="v", tag="v", bufs=4)
            for c in range(PACK):
                n_tile = PACK * part + c
                nc.scalar.activation(
                    out=v[i][:, c, :], in_=sums[i, c // 2][:, c % 2, :], func=ACT.Relu,
                    bias=b2_col[:, n_tile : n_tile + 1], scale=1.0,
                )

        def pe_out(i):
            pair, r = divmod(i, 2)
            for g in range(PASSES):
                out_ps[i, g] = psum.tile([P, BANK], F32, name="out_ps", tag="out", bufs=2)
                for c in range(PACK):
                    nc.tensor.transpose(
                        out_ps[i, g][:, c * P : (c + 1) * P], v[2 * pair + g][:, c, r * P : (r + 1) * P], ident_f32[:]
                    )

        def finish(i):
            chunk, r = divmod(i, ROWS)
            out_rows = sbuf.tile([P, HIDDEN], F32, name="out_rows", tag="out_rows", bufs=6)
            for g in range(PASSES):
                cols = slice(g * BANK, (g + 1) * BANK)
                nc.vector.scalar_tensor_tensor(
                    out=out_rows[:, cols], in0=z[i][:, cols], scalar=0.0, in1=out_ps[i, g][:],
                    op0=ALU.max, op1=ALU.add,
                )
            nc.sync.dma_start(out=out_chunks[chunk][:, r, :], in_=out_rows[:])

        def run(stage, step, lag):
            if 0 <= step - lag < TILES:
                stage(step - lag)

        def warm(count):
            for d in range(count):
                ps = psum.tile([P, BANK], F32, name="warm_ps", tag="out", bufs=2)
                nc.tensor.matmul(ps[:], lhsT=ones[:], rhs=zeros[:], start=True, stop=True)

        warm(4)
        for step in range(TILES + LAST_LAG):
            if step % ROWS == 0 and step // ROWS + LOAD_AHEAD < CHUNKS:
                load_x(step // ROWS + LOAD_AHEAD)
            if step < 4:
                warm(2)
            if step == 1:
                spread_feat_b()
                turn_trans_b()
            run(round_h, step, 2)
            run(pe_mix, step, 6)
            run(relu_sums, step, 6)
            run(quantise, step, 4)
            run(pe_out, step, 8)
            run(finish, step, 8)
            run(pe_layer, step, 1)
            run(add_bias, step, 1)
            run(pe_x, step, 0)
            run(copy_x, step, 0)
            run(pe_turn, step, 2)
            run(copy_h, step, 2)
            if step == 1:
                regroup_w(0, 0, "S")
                regroup_w(0, 1, "V")
            if step == 2:
                regroup_w(1, 0, "S")
                regroup_w(1, 1, "V")
            if step == 3:
                quantise_w(0, 0)
                quantise_w(0, 1)
            if step == 4:
                quantise_w(1, 0)
                quantise_w(1, 1)
